import numpy as np
import ml_dtypes


def mxq(x, axis, fmt="e4m3"):
    dtype, down = {"e4m3": (ml_dtypes.float8_e4m3fn, 7), "e5m2": (ml_dtypes.float8_e5m2, 14)}[fmt]
    v = np.moveaxis(np.asarray(x, np.float32).astype(ml_dtypes.bfloat16).astype(np.float64), axis, -1)
    blocks = v.reshape(v.shape[:-1] + (-1, 32))
    amax = np.abs(blocks).max(-1, keepdims=True)
    byte = np.maximum(np.where(amax > 0, np.frexp(amax)[1] - 1 + 127, 0) - down, 1)
    scale = np.exp2(byte - 127.0)
    codes = (blocks / scale).astype(np.float32).astype(dtype).astype(np.float64)
    return np.moveaxis((codes * scale).reshape(v.shape), -1, axis)


WIDE = False


def mx_kscale(k):
    if not WIDE:
        return np.ones(k)
    levels = np.array([10, -10, 5, -5, 0])
    a = np.random.permutation(np.resize(levels, k // 512 * 4)).reshape(k // 512, 4)
    idx = np.arange(k)
    return np.exp2(a[idx // 512, idx % 128 // 32])


BF16 = ml_dtypes.bfloat16


def bf(x):
    return np.asarray(x, np.float32).astype(BF16)


def f64(x):
    return np.asarray(x).astype(np.float64)


B, L, C, H, W, HID = 1, 5, 128, 32, 16, 8192


def silu(v):
    return v / (1.0 + np.exp(-v))


def _dwt(x):
    x1 = x[:, :, 0::2, 0::2] * 0.5
    x2 = x[:, :, 1::2, 0::2] * 0.5
    x3 = x[:, :, 0::2, 1::2] * 0.5
    x4 = x[:, :, 1::2, 1::2] * 0.5
    return np.concatenate([x1 + x2 + x3 + x4,
                           -x1 - x2 + x3 + x4,
                           -x1 + x2 - x3 + x4,
                           x1 - x2 - x3 + x4], axis=1)


def _idwt(y):
    n, c4, hh, wh = y.shape
    co = c4 // 4
    y1 = y[:, 0 * co:1 * co] * 0.5
    y2 = y[:, 1 * co:2 * co] * 0.5
    y3 = y[:, 2 * co:3 * co] * 0.5
    y4 = y[:, 3 * co:4 * co] * 0.5
    a = y1 - y2 - y3 + y4
    b = y1 - y2 + y3 - y4
    c = y1 + y2 - y3 - y4
    d = y1 + y2 + y3 + y4
    r0 = np.stack([a, c], axis=-1).reshape(n, co, hh, 2 * wh)
    r1 = np.stack([b, d], axis=-1).reshape(n, co, hh, 2 * wh)
    return np.stack([r0, r1], axis=-2).reshape(n, co, 2 * hh, 2 * wh)


def setup_inputs():
    s = mx_kscale(4 * C)[:C]
    s4 = np.tile(s, 4)
    return {"x": bf(np.random.standard_normal((B, L, C, H, W)) * s[:, None, None]),
            "conv_w": bf(np.random.standard_normal((HID, 4 * C)) / np.sqrt(4 * C) / s4[None, :]),
            "conv_b": bf(np.random.standard_normal(HID) * 0.3),
            "conv_out_w": bf(np.random.standard_normal((4 * C, HID)) * 1.5 / np.sqrt(HID)),
            "conv_out_b": bf(np.random.standard_normal(4 * C) * 0.3)}


def reference(x, conv_w, conv_b, conv_out_w, conv_out_b):
    x = f64(x)
    b, l, c, h, w = x.shape
    pad_h = (2 - h % 2) % 2
    pad_w = (2 - w % 2) % 2
    if pad_h > 0 or pad_w > 0:
        x = np.pad(x, ((0, 0), (0, 0), (0, 0), (0, pad_h), (0, pad_w)))
    hp, wp = x.shape[-2], x.shape[-1]
    xf = x.reshape(b * l, c, hp, wp)
    x_dwt = _dwt(xf)
    n, c4, hh, wh = x_dwt.shape
    xq = mxq(x_dwt, 1, "e4m3").reshape(n, c4, hh * wh)
    feat = (mxq(f64(conv_w), 1, "e4m3") @ xq) + f64(conv_b)[None, :, None]
    feat = silu(feat)
    y = (mxq(f64(conv_out_w), 1, "e4m3") @ mxq(feat, 1, "e4m3")) + f64(conv_out_b)[None, :, None]
    rec = _idwt(y.reshape(n, c4, hh, wh))
    out = rec.reshape(b, l, c, hp, wp)
    if pad_h > 0 or pad_w > 0:
        out = out[..., :h, :w]
    return out

@@ -1,0 +1,356 @@
+from contextlib import ExitStack
+
+import concourse.mybir as mybir
+from concourse.masks import make_identity
+
+F32 = mybir.dt.float32
+BF16 = mybir.dt.bfloat16
+U32 = mybir.dt.uint32
+U8 = mybir.dt.uint8
+FP8X4 = mybir.dt.float8_e4m3fn_x4
+ALU = mybir.AluOpType
+FUNC = mybir.ActivationFunctionType
+
+P = 128
+PACK = 4
+K_PASS = P * PACK
+FRAMES = 5
+FRAME_PIX = 128
+PIX = FRAMES * FRAME_PIX
+PIX_MAIN = 4 * FRAME_PIX
+WAVE = 512
+HID = 8192
+GROUPS = HID // K_PASS
+RAW_BUFS = 6
+LEAD = 3
+
+FLOPS = 2 * 2 * HID * WAVE * PIX
+
+
+def tile_waveletblock_k_kernel(tc, x, conv_w, conv_b, conv_out_w, conv_out_b, out):
+    nc = tc.nc
+    with ExitStack() as ctx:
+        ctx.enter_context(tc.manual_schedule())
+        keep = ctx.enter_context(tc.tile_pool(name="keep", bufs=1))
+        raw = ctx.enter_context(tc.tile_pool(name="raw", bufs=RAW_BUFS))
+        ahead_pool = ctx.enter_context(tc.tile_pool(name="ahead", bufs=LEAD + 1))
+        stage = ctx.enter_context(tc.tile_pool(name="stage", bufs=2))
+        acc = ctx.enter_context(tc.psum_pool(name="acc", bufs=1))
+        work = ctx.enter_context(tc.psum_pool(name="work", bufs=4))
+
+        d_grouped = keep.tile([P, PIX * PACK], BF16, align_bytes=64)
+        d_codes = keep.tile([P, PIX], U32, align_bytes=64)
+        d_scales = keep.tile([P, PIX], U8, align_bytes=64)
+        w2_codes = keep.tile([P, GROUPS, K_PASS], U32, align_bytes=64)
+        w2_scales = keep.tile([P, GROUPS, K_PASS], U8, align_bytes=64)
+        rest_codes = keep.tile([P, GROUPS, FRAME_PIX], U32, align_bytes=64)
+        rest_scales = keep.tile([P, GROUPS, FRAME_PIX], U8, align_bytes=64)
+
+        w1_view = conv_w.rearrange("(g u j e) k -> g j u (e k)", u=2, j=P, e=2)
+        w2_view = conv_out_w.rearrange("(s m) (g o) -> g m s o", m=P, o=K_PASS)
+        w1_words = {}
+        w2_words = {}
+
+        def load_weights(g):
+            if g >= GROUPS:
+                return
+            w1_raw = raw.tile([P, 2, 2 * WAVE], BF16, tag="w1_raw")
+            nc.sync.dma_start(out=w1_raw[:], in_=w1_view[g])
+            w2_raw = raw.tile([P, 4, K_PASS], BF16, tag="w2_raw")
+            nc.sync.dma_start(out=w2_raw[:], in_=w2_view[g])
+            w1_words[g] = w1_raw[:].bitcast(F32)
+            w2_words[g] = w2_raw[:].bitcast(F32)
+
+        x_view = x.rearrange("b l (q e) h w -> q (b l) (e h w)", e=2)
+        x_sb = keep.tile([P, FRAMES, 2 * 512], BF16)
+        nc.sync.dma_start(out=x_sb[0:64], in_=x_view)
+        hid_bias_rows = keep.tile([P, 2 * P], BF16)
+        out_bias_rows = keep.tile([P, P], BF16)
+        nc.vector.memset(hid_bias_rows[:], 0.0)
+        nc.vector.memset(out_bias_rows[:], 0.0)
+        nc.scalar.dma_start(out=hid_bias_rows[0:32, :], in_=conv_b.rearrange("(r c) -> r c", c=2 * P))
+        nc.scalar.dma_start(out=out_bias_rows[0:4, :], in_=conv_out_b.rearrange("(s c) -> s c", c=P))
+        nc.scalar.dma_start(out=x_sb[64:128], in_=x_view)
+        for g in range(RAW_BUFS):
+            load_weights(g)
+
+        ident = keep.tile([P, P], F32)
+        make_identity(nc, ident[:])
+        sign = keep.tile([P, 1], F32)
+        nc.vector.memset(sign[0:64], 1.0)
+        nc.vector.memset(sign[64:128], -1.0)
+        zero = keep.tile([P, 1], F32)
+        nc.vector.memset(zero[:], 0.0)
+        warm = keep.tile([P, 1], F32)
+        nc.scalar.activation(out=warm[:], in_=zero[:], func=FUNC.Silu)
+
+        bias_f32 = keep.tile([P, 3, P], F32)
+        nc.vector.tensor_copy(
+            out=bias_f32[:, 0:2, :], in_=hid_bias_rows[:].rearrange("r (j e) -> r e j", e=2)
+        )
+        nc.vector.tensor_copy(out=bias_f32[:, 2, :], in_=out_bias_rows[:])
+        bias_bank = work.tile([P, 3, P], F32, tag="work")
+        for i in range(3):
+            nc.tensor.transpose(bias_bank[:, i, :], bias_f32[:, i, :], ident[:])
+        hid_bias = keep.tile([P, 4 * GROUPS], F32)
+        nc.vector.tensor_copy(
+            out=hid_bias[:].rearrange("j (r e) -> j r e", e=2),
+            in_=bias_bank[:, 0:2, 0 : 2 * GROUPS].rearrange("j e r -> j r e"),
+        )
+        out_bias_half = keep.tile([P, 4], F32)
+        nc.vector.tensor_scalar_mul(out=out_bias_half[:], in0=bias_bank[:, 2, 0:4], scalar1=0.5)
+
+        with tc.tile_pool(name="head", bufs=1) as head:
+            x_cols = x_sb[:].rearrange("p l (n b) -> p (l n) b", b=2)
+            col_step = head.tile([P, FRAMES * 2 * 256], F32)
+            nc.vector.scalar_tensor_tensor(
+                out=col_step[:],
+                in0=x_cols[:, :, 0],
+                scalar=sign[:, 0:1],
+                in1=x_cols[:, :, 1],
+                op0=ALU.mult,
+                op1=ALU.add,
+            )
+            rows = col_step[:].rearrange("p (l e i a j) -> p l e i a j", l=FRAMES, e=2, i=16, a=2)
+            twice_d = head.tile([P, 2, 2, FRAMES, FRAME_PIX], F32)
+            for u, op in ((0, ALU.add), (1, ALU.subtract)):
+                nc.vector.tensor_tensor(
+                    out=twice_d[:, u].rearrange("p e l (i j) -> p l e i j", j=8),
+                    in0=rows[:, :, :, :, 1, :],
+                    in1=rows[:, :, :, :, 0, :],
+                    op=op,
+                )
+            nc.vector.tensor_scalar_mul(
+                out=d_grouped[:].rearrange("p (n t) -> p n t", t=PACK),
+                in0=twice_d[:].rearrange("p u e l n -> p (l n) (u e)"),
+                scalar1=0.5,
+            )
+        for first, last in ((0, PIX_MAIN), (PIX_MAIN, PIX)):
+            nc.vector.quantize_mx(
+                out=d_codes[:, first:last].bitcast(FP8X4),
+                scales=d_scales[:, first:last],
+                in_=d_grouped[:, PACK * first : PACK * last],
+            )
+
+        w1_grouped = {}
+        w2_grouped = {}
+        w1_codes = {}
+        w1_scales = {}
+        hidden = {}
+        f_grouped = {}
+        f_codes = {}
+        f_scales = {}
+        y_main = [acc.tile([P, PIX_MAIN], F32, name="y_main%d" % s) for s in range(4)]
+
+        def exists(g):
+            return 0 <= g < GROUPS
+
+        def transpose_weights(g):
+            if not exists(g):
+                return
+            w1_grouped[g] = ahead_pool.tile([P, K_PASS * PACK], BF16, tag="w1_grouped", name="w1_grouped", align_bytes=64)
+            w2_grouped[g] = ahead_pool.tile([P, K_PASS * PACK], BF16, tag="w2_grouped", name="w2_grouped", align_bytes=64)
+            w1_pairs = w1_grouped[g][:].bitcast(F32).rearrange("p (c u) -> p c u", u=2)
+            w2_pairs = w2_grouped[g][:].bitcast(F32).rearrange("p (c u) -> p c u", u=2)
+            for half in range(2):
+                bank = work.tile([P, 2, 2, P], F32, tag="work")
+                for u in range(2):
+                    for e in range(2):
+                        first = 256 * e + P * u
+                        nc.tensor.transpose(
+                            bank[:, u, e, :], w1_words[g][:, half, first : first + P], ident[:]
+                        )
+                nc.scalar.copy(
+                    out=w1_pairs[:, 256 * half : 256 * half + 256, :],
+                    in_=bank[:].rearrange("p u e j -> p (e j) u"),
+                )
+            for half in range(2):
+                bank = work.tile([P, 2, 2, P], F32, tag="work")
+                for u in range(2):
+                    for s in range(2):
+                        nc.tensor.transpose(
+                            bank[:, u, s, :], w2_words[g][:, 2 * half + s, P * u : P * u + P], ident[:]
+                        )
+                if half == 0 or g < LEAD:
+                    nc.scalar.copy(
+                        out=w2_pairs[:, 256 * half : 256 * half + 256, :],
+                        in_=bank[:].rearrange("p u s m -> p (s m) u"),
+                    )
+                else:
+                    nc.vector.tensor_copy(
+                        out=w2_pairs[:, 256 * half : 256 * half + 256, :],
+                        in_=bank[:].rearrange("p u s m -> p (s m) u"),
+                    )
+            load_weights(g + RAW_BUFS)
+
+        def quantise_w1(g):
+            if not exists(g):
+                return
+            w1_codes[g] = ahead_pool.tile([P, K_PASS], U32, tag="w1_codes", name="w1_codes", align_bytes=64)
+            w1_scales[g] = ahead_pool.tile([P, K_PASS], U8, tag="w1_scales", name="w1_scales", align_bytes=64)
+            nc.vector.quantize_mx(
+                out=w1_codes[g][:].bitcast(FP8X4), scales=w1_scales[g][:], in_=w1_grouped[g][:]
+            )
+
+        def quantise_w2(g):
+            if not exists(g):
+                return
+            nc.vector.quantize_mx(
+                out=w2_codes[:, g, :].bitcast(FP8X4), scales=w2_scales[:, g, :], in_=w2_grouped[g][:]
+            )
+
+        def hidden_main(g, chunks):
+            if not exists(g):
+                return
+            if g not in hidden:
+                hidden[g] = stage.tile([P, PACK, PIX], BF16, tag="hidden", name="hidden")
+            for t in chunks:
+                bank = work.tile([P, PIX_MAIN], F32, tag="work")
+                nc.tensor.matmul_mx(
+                    out=bank[:],
+                    lhsT=w1_codes[g][:, P * t : P * t + P].bitcast(FP8X4),
+                    lhsT_scale=w1_scales[g][:, P * t : P * t + P],
+                    rhs=d_codes[:, 0:PIX_MAIN].bitcast(FP8X4),
+                    rhs_scale=d_scales[:, 0:PIX_MAIN],
+                    start=True,
+                    stop=True,
+                )
+                nc.scalar.activation(
+                    out=hidden[g][:, t, 0:PIX_MAIN],
+                    in_=bank[:],
+                    func=FUNC.Silu,
+                    bias=hid_bias[:, PACK * g + t : PACK * g + t + 1],
+                    scale=1.0,
+                )
+
+        def hidden_rest(g):
+            if not exists(g):
+                return
+            bank = work.tile([P, PACK, FRAME_PIX], F32, tag="work")
+            for t in range(PACK):
+                nc.tensor.matmul_mx(
+                    out=bank[:, t, :],
+                    lhsT=w1_codes[g][:, P * t : P * t + P].bitcast(FP8X4),
+                    lhsT_scale=w1_scales[g][:, P * t : P * t + P],
+                    rhs=d_codes[:, PIX_MAIN:PIX].bitcast(FP8X4),
+                    rhs_scale=d_scales[:, PIX_MAIN:PIX],
+                    start=True,
+                    stop=True,
+                )
+            for t in range(PACK):
+                nc.scalar.activation(
+                    out=hidden[g][:, t, PIX_MAIN:PIX],
+                    in_=bank[:, t, :],
+                    func=FUNC.Silu,
+                    bias=hid_bias[:, PACK * g + t : PACK * g + t + 1],
+                    scale=1.0,
+                )
+
+        def regroup(g, first, last):
+            if not exists(g):
+                return
+            if g not in f_grouped:
+                f_grouped[g] = stage.tile([P, PIX * PACK], BF16, tag="f_grouped", name="f_grouped", align_bytes=64)
+            nc.vector.tensor_copy(
+                out=f_grouped[g][:, PACK * first : PACK * last].rearrange("p (c i t) -> p c t i", i=4, t=PACK),
+                in_=hidden[g][:, :, first:last].rearrange("p t (c i) -> p c t i", i=4),
+            )
+
+        def quantise_main(g):
+            if not exists(g):
+                return
+            f_codes[g] = stage.tile([P, PIX_MAIN], U32, tag="f_codes", name="f_codes", align_bytes=64)
+            f_scales[g] = stage.tile([P, PIX_MAIN], U8, tag="f_scales", name="f_scales", align_bytes=64)
+            nc.vector.quantize_mx(
+                out=f_codes[g][:].bitcast(FP8X4),
+                scales=f_scales[g][:],
+                in_=f_grouped[g][:, 0 : PACK * PIX_MAIN],
+            )
+
+        def quantise_rest(g):
+            if not exists(g):
+                return
+            nc.vector.quantize_mx(
+                out=rest_codes[:, g, :].bitcast(FP8X4),
+                scales=rest_scales[:, g, :],
+                in_=f_grouped[g][:, PACK * PIX_MAIN : PACK * PIX],
+            )
+
+        def output_main(g, subbands):
+            if not exists(g):
+                return
+            for s in subbands:
+                nc.tensor.matmul_mx(
+                    out=y_main[s][:],
+                    lhsT=w2_codes[:, g, P * s : P * s + P].bitcast(FP8X4),
+                    lhsT_scale=w2_scales[:, g, P * s : P * s + P],
+                    rhs=f_codes[g][:].bitcast(FP8X4),
+                    rhs_scale=f_scales[g][:],
+                    start=(g == 0),
+                    stop=(g == GROUPS - 1),
+                )
+
+        for step in range(-LEAD, GROUPS + 1):
+            regroup(step - 1, 0, PIX_MAIN)
+            transpose_weights(step + LEAD)
+            quantise_main(step - 1)
+            hidden_main(step, (0, 1))
+            output_main(step - 1, (0, 1))
+            regroup(step - 1, PIX_MAIN, PIX)
+            quantise_w1(step + LEAD)
+            quantise_rest(step - 1)
+            quantise_w2(step + LEAD)
+            hidden_main(step, (2, 3))
+            output_main(step - 1, (2, 3))
+            hidden_rest(step)
+
+        y_rest = work.tile([P, 4, FRAME_PIX], F32, tag="work")
+        for s in range(4):
+            for g in range(GROUPS):
+                nc.tensor.matmul_mx(
+                    out=y_rest[:, s, :],
+                    lhsT=w2_codes[:, g, P * s : P * s + P].bitcast(FP8X4),
+                    lhsT_scale=w2_scales[:, g, P * s : P * s + P],
+                    rhs=rest_codes[:, g, :].bitcast(FP8X4),
+                    rhs_scale=rest_scales[:, g, :],
+                    start=(g == 0),
+                    stop=(g == GROUPS - 1),
+                )
+
+        tail = ctx.enter_context(tc.tile_pool(name="tail", bufs=1))
+        z = tail.tile([P, 4, PIX], F32)
+        low = tail.tile([P, 2, PIX], F32)
+        high = tail.tile([P, 2, PIX], F32)
+        image = tail.tile([P, FRAMES * 16, 2, 16], F32)
+        out_view = out.rearrange("b l c h w -> c (b l) (h w)")
+        image_view = image[:].rearrange("c (l i) a w -> c l (i a w)", l=FRAMES)
+
+        def finish(first_frame, last_frame, banks):
+            pix = slice(FRAME_PIX * first_frame, FRAME_PIX * last_frame)
+            lines = slice(16 * first_frame, 16 * last_frame)
+            for s in (2, 3, 0, 1):
+                nc.scalar.activation(
+                    out=z[:, s, pix],
+                    in_=banks[s],
+                    func=FUNC.Identity,
+                    bias=out_bias_half[:, s : s + 1],
+                    scale=0.5,
+                )
+            for pair, first in ((high, 2), (low, 0)):
+                nc.vector.tensor_sub(out=pair[:, 0, pix], in0=z[:, first, pix], in1=z[:, first + 1, pix])
+                nc.vector.tensor_add(out=pair[:, 1, pix], in0=z[:, first, pix], in1=z[:, first + 1, pix])
+            low_jb = low[:, :, pix].rearrange("c b (n j) -> c n j b", j=8)
+            high_jb = high[:, :, pix].rearrange("c b (n j) -> c n j b", j=8)
+            for a, op in ((0, ALU.subtract), (1, ALU.add)):
+                nc.vector.tensor_tensor(
+                    out=image[:, lines, a, :].rearrange("c n (j b) -> c n j b", b=2),
+                    in0=low_jb,
+                    in1=high_jb,
+                    op=op,
+                )
+            nc.sync.dma_start(
+                out=out_view[:, first_frame:last_frame, :], in_=image_view[:, first_frame:last_frame, :]
+            )
+
+        finish(0, 4, [y_main[s][:] for s in range(4)])
+        finish(4, 5, [y_rest[:, s, :] for s in range(4)])

@@ -63,14 +63,14 @@ def tile_waveletblock_k_kernel(tc, x, conv_w, conv_b, conv_out_w, conv_out_b, ou
 
         x_view = x.rearrange("b l (q e) h w -> q (b l) (e h w)", e=2)
         x_sb = keep.tile([P, FRAMES, 2 * 512], BF16)
-        nc.sync.dma_start(out=x_sb[0:64], in_=x_view)
         hid_bias_rows = keep.tile([P, 2 * P], BF16)
         out_bias_rows = keep.tile([P, P], BF16)
         nc.vector.memset(hid_bias_rows[:], 0.0)
         nc.vector.memset(out_bias_rows[:], 0.0)
-        nc.scalar.dma_start(out=hid_bias_rows[0:32, :], in_=conv_b.rearrange("(r c) -> r c", c=2 * P))
-        nc.scalar.dma_start(out=out_bias_rows[0:4, :], in_=conv_out_b.rearrange("(s c) -> s c", c=P))
         nc.scalar.dma_start(out=x_sb[64:128], in_=x_view)
+        nc.sync.dma_start(out=x_sb[0:64], in_=x_view)
+        nc.sync.dma_start(out=hid_bias_rows[0:32, :], in_=conv_b.rearrange("(r c) -> r c", c=2 * P))
+        nc.sync.dma_start(out=out_bias_rows[0:4, :], in_=conv_out_b.rearrange("(s c) -> s c", c=P))
         for g in range(RAW_BUFS):
             load_weights(g)
 
@@ -203,7 +203,7 @@ def tile_waveletblock_k_kernel(tc, x, conv_w, conv_b, conv_out_w, conv_out_b, ou
             if not exists(g):
                 return
             if g not in hidden:
-                hidden[g] = stage.tile([P, PACK, PIX], BF16, tag="hidden", name="hidden")
+                hidden[g] = stage.tile([P, PACK, PIX], BF16, tag="hidden", name="hidden", bufs=3)
             for t in chunks:
                 bank = work.tile([P, PIX_MAIN], F32, tag="work")
                 nc.tensor.matmul_mx(
@@ -259,8 +259,8 @@ def tile_waveletblock_k_kernel(tc, x, conv_w, conv_b, conv_out_w, conv_out_b, ou
         def quantise_main(g):
             if not exists(g):
                 return
-            f_codes[g] = stage.tile([P, PIX_MAIN], U32, tag="f_codes", name="f_codes", align_bytes=64)
-            f_scales[g] = stage.tile([P, PIX_MAIN], U8, tag="f_scales", name="f_scales", align_bytes=64)
+            f_codes[g] = stage.tile([P, PIX_MAIN], U32, tag="f_codes", name="f_codes", bufs=3, align_bytes=64)
+            f_scales[g] = stage.tile([P, PIX_MAIN], U8, tag="f_scales", name="f_scales", bufs=3, align_bytes=64)
             nc.vector.quantize_mx(
                 out=f_codes[g][:].bitcast(FP8X4),
                 scales=f_scales[g][:],
@@ -290,18 +290,18 @@ def tile_waveletblock_k_kernel(tc, x, conv_w, conv_b, conv_out_w, conv_out_b, ou
                     stop=(g == GROUPS - 1),
                 )
 
-        for step in range(-LEAD, GROUPS + 1):
+        for step in range(-LEAD, GROUPS + 2):
             regroup(step - 1, 0, PIX_MAIN)
             transpose_weights(step + LEAD)
             quantise_main(step - 1)
             hidden_main(step, (0, 1))
-            output_main(step - 1, (0, 1))
+            output_main(step - 2, (0, 1))
             regroup(step - 1, PIX_MAIN, PIX)
             quantise_w1(step + LEAD)
             quantise_rest(step - 1)
             quantise_w2(step + LEAD)
             hidden_main(step, (2, 3))
-            output_main(step - 1, (2, 3))
+            output_main(step - 2, (2, 3))
             hidden_rest(step)
 
         y_rest = work.tile([P, 4, FRAME_PIX], F32, tag="work")

@@ -23,6 +23,7 @@ HID = 8192
 GROUPS = HID // K_PASS
 RAW_BUFS = 6
 LEAD = 3
+LAG = 2
 
 FLOPS = 2 * 2 * HID * WAVE * PIX
 
@@ -33,8 +34,8 @@ def tile_waveletblock_k_kernel(tc, x, conv_w, conv_b, conv_out_w, conv_out_b, ou
         ctx.enter_context(tc.manual_schedule())
         keep = ctx.enter_context(tc.tile_pool(name="keep", bufs=1))
         raw = ctx.enter_context(tc.tile_pool(name="raw", bufs=RAW_BUFS))
-        ahead_pool = ctx.enter_context(tc.tile_pool(name="ahead", bufs=LEAD + 1))
-        stage = ctx.enter_context(tc.tile_pool(name="stage", bufs=2))
+        ahead = ctx.enter_context(tc.tile_pool(name="ahead", bufs=LEAD + 1))
+        stage = ctx.enter_context(tc.tile_pool(name="stage", bufs=LAG + 1))
         acc = ctx.enter_context(tc.psum_pool(name="acc", bufs=1))
         work = ctx.enter_context(tc.psum_pool(name="work", bufs=4))
 
@@ -45,6 +46,18 @@ def tile_waveletblock_k_kernel(tc, x, conv_w, conv_b, conv_out_w, conv_out_b, ou
         w2_scales = keep.tile([P, GROUPS, K_PASS], U8, align_bytes=64)
         rest_codes = keep.tile([P, GROUPS, FRAME_PIX], U32, align_bytes=64)
         rest_scales = keep.tile([P, GROUPS, FRAME_PIX], U8, align_bytes=64)
+
+        hid_bias_rows = keep.tile([P, 2 * P], BF16)
+        out_bias_rows = keep.tile([P, P], BF16)
+        nc.vector.memset(hid_bias_rows[:], 0.0)
+        nc.vector.memset(out_bias_rows[:], 0.0)
+        nc.sync.dma_start(out=hid_bias_rows[0 : 2 * GROUPS, :], in_=conv_b.rearrange("(r c) -> r c", c=2 * P))
+        nc.sync.dma_start(out=out_bias_rows[0:4, :], in_=conv_out_b.rearrange("(s c) -> s c", c=P))
+        x_view = x.rearrange("b l (q e) h w -> q (b l) (e h w)", e=2)
+        x_sb = keep.tile([P, FRAMES, 2 * 512], BF16)
+        for frame in range(FRAMES):
+            nc.sync.dma_start(out=x_sb[0:64, frame, :], in_=x_view[:, frame, :])
+            nc.scalar.dma_start(out=x_sb[64:128, frame, :], in_=x_view[:, frame, :])
 
         w1_view = conv_w.rearrange("(g u j e) k -> g j u (e k)", u=2, j=P, e=2)
         w2_view = conv_out_w.rearrange("(s m) (g o) -> g m s o", m=P, o=K_PASS)
@@ -61,16 +74,6 @@ def tile_waveletblock_k_kernel(tc, x, conv_w, conv_b, conv_out_w, conv_out_b, ou
             w1_words[g] = w1_raw[:].bitcast(F32)
             w2_words[g] = w2_raw[:].bitcast(F32)
 
-        x_view = x.rearrange("b l (q e) h w -> q (b l) (e h w)", e=2)
-        x_sb = keep.tile([P, FRAMES, 2 * 512], BF16)
-        hid_bias_rows = keep.tile([P, 2 * P], BF16)
-        out_bias_rows = keep.tile([P, P], BF16)
-        nc.vector.memset(hid_bias_rows[:], 0.0)
-        nc.vector.memset(out_bias_rows[:], 0.0)
-        nc.scalar.dma_start(out=x_sb[64:128], in_=x_view)
-        nc.sync.dma_start(out=x_sb[0:64], in_=x_view)
-        nc.sync.dma_start(out=hid_bias_rows[0:32, :], in_=conv_b.rearrange("(r c) -> r c", c=2 * P))
-        nc.sync.dma_start(out=out_bias_rows[0:4, :], in_=conv_out_b.rearrange("(s c) -> s c", c=P))
         for g in range(RAW_BUFS):
             load_weights(g)
 
@@ -92,26 +95,27 @@ def tile_waveletblock_k_kernel(tc, x, conv_w, conv_b, conv_out_w, conv_out_b, ou
         bias_bank = work.tile([P, 3, P], F32, tag="work")
         for i in range(3):
             nc.tensor.transpose(bias_bank[:, i, :], bias_f32[:, i, :], ident[:])
-        hid_bias = keep.tile([P, 4 * GROUPS], F32)
-        nc.vector.tensor_copy(
-            out=hid_bias[:].rearrange("j (r e) -> j r e", e=2),
-            in_=bias_bank[:, 0:2, 0 : 2 * GROUPS].rearrange("j e r -> j r e"),
-        )
-        out_bias_half = keep.tile([P, 4], F32)
-        nc.vector.tensor_scalar_mul(out=out_bias_half[:], in0=bias_bank[:, 2, 0:4], scalar1=0.5)
 
+        hid_bias = keep.tile([P, PACK * GROUPS], F32)
+        out_bias_half = keep.tile([P, 4], F32)
         with tc.tile_pool(name="head", bufs=1) as head:
-            x_cols = x_sb[:].rearrange("p l (n b) -> p (l n) b", b=2)
-            col_step = head.tile([P, FRAMES * 2 * 256], F32)
-            nc.vector.scalar_tensor_tensor(
-                out=col_step[:],
-                in0=x_cols[:, :, 0],
-                scalar=sign[:, 0:1],
-                in1=x_cols[:, :, 1],
-                op0=ALU.mult,
-                op1=ALU.add,
+            col_step = head.tile([P, FRAMES, 2 * 256], F32)
+            for frame in range(FRAMES):
+                x_cols = x_sb[:, frame, :].rearrange("p (n b) -> p n b", b=2)
+                nc.vector.scalar_tensor_tensor(
+                    out=col_step[:, frame, :],
+                    in0=x_cols[:, :, 0],
+                    scalar=sign[:, 0:1],
+                    in1=x_cols[:, :, 1],
+                    op0=ALU.mult,
+                    op1=ALU.add,
+                )
+            nc.vector.tensor_copy(
+                out=hid_bias[:].rearrange("j (r e) -> j r e", e=2),
+                in_=bias_bank[:, 0:2, 0 : 2 * GROUPS].rearrange("j e r -> j r e"),
             )
-            rows = col_step[:].rearrange("p (l e i a j) -> p l e i a j", l=FRAMES, e=2, i=16, a=2)
+            nc.vector.tensor_scalar_mul(out=out_bias_half[:], in0=bias_bank[:, 2, 0:4], scalar1=0.5)
+            rows = col_step[:].rearrange("p l (e i a j) -> p l e i a j", e=2, i=16, a=2)
             twice_d = head.tile([P, 2, 2, FRAMES, FRAME_PIX], F32)
             for u, op in ((0, ALU.add), (1, ALU.subtract)):
                 nc.vector.tensor_tensor(
@@ -145,49 +149,44 @@ def tile_waveletblock_k_kernel(tc, x, conv_w, conv_b, conv_out_w, conv_out_b, ou
         def exists(g):
             return 0 <= g < GROUPS
 
-        def transpose_weights(g):
+        def transpose_512_columns(block, grouped, vector_helps):
+            pairs = grouped[:].bitcast(F32).rearrange("p (c u) -> p c u", u=2)
+            for half in range(2):
+                bank = work.tile([P, 2, 2, P], F32, tag="work")
+                for u in range(2):
+                    for c in range(2):
+                        nc.tensor.transpose(bank[:, u, c, :], block(half, u, c), ident[:])
+                dst = pairs[:, 256 * half : 256 * half + 256, :]
+                src = bank[:].rearrange("p u c j -> p (c j) u")
+                if half == 1 and vector_helps:
+                    nc.vector.tensor_copy(out=dst, in_=src)
+                else:
+                    nc.scalar.copy(out=dst, in_=src)
+
+        def transpose_w1(g):
             if not exists(g):
                 return
-            w1_grouped[g] = ahead_pool.tile([P, K_PASS * PACK], BF16, tag="w1_grouped", name="w1_grouped", align_bytes=64)
-            w2_grouped[g] = ahead_pool.tile([P, K_PASS * PACK], BF16, tag="w2_grouped", name="w2_grouped", align_bytes=64)
-            w1_pairs = w1_grouped[g][:].bitcast(F32).rearrange("p (c u) -> p c u", u=2)
-            w2_pairs = w2_grouped[g][:].bitcast(F32).rearrange("p (c u) -> p c u", u=2)
-            for half in range(2):
-                bank = work.tile([P, 2, 2, P], F32, tag="work")
-                for u in range(2):
-                    for e in range(2):
-                        first = 256 * e + P * u
-                        nc.tensor.transpose(
-                            bank[:, u, e, :], w1_words[g][:, half, first : first + P], ident[:]
-                        )
-                nc.scalar.copy(
-                    out=w1_pairs[:, 256 * half : 256 * half + 256, :],
-                    in_=bank[:].rearrange("p u e j -> p (e j) u"),
-                )
-            for half in range(2):
-                bank = work.tile([P, 2, 2, P], F32, tag="work")
-                for u in range(2):
-                    for s in range(2):
-                        nc.tensor.transpose(
-                            bank[:, u, s, :], w2_words[g][:, 2 * half + s, P * u : P * u + P], ident[:]
-                        )
-                if half == 0 or g < LEAD:
-                    nc.scalar.copy(
-                        out=w2_pairs[:, 256 * half : 256 * half + 256, :],
-                        in_=bank[:].rearrange("p u s m -> p (s m) u"),
-                    )
-                else:
-                    nc.vector.tensor_copy(
-                        out=w2_pairs[:, 256 * half : 256 * half + 256, :],
-                        in_=bank[:].rearrange("p u s m -> p (s m) u"),
-                    )
+            w1_grouped[g] = ahead.tile([P, K_PASS * PACK], BF16, tag="w1_grouped", name="w1_grouped", align_bytes=64)
+            words = w1_words[g]
+            transpose_512_columns(
+                lambda half, u, e: words[:, half, 256 * e + P * u : 256 * e + P * u + P], w1_grouped[g], g >= LEAD
+            )
+
+        def transpose_w2(g):
+            if not exists(g):
+                return
+            w2_grouped[g] = ahead.tile([P, K_PASS * PACK], BF16, tag="w2_grouped", name="w2_grouped", align_bytes=64)
+            words = w2_words[g]
+            transpose_512_columns(
+                lambda half, u, s: words[:, 2 * half + s, P * u : P * u + P], w2_grouped[g], g >= LEAD
+            )
             load_weights(g + RAW_BUFS)
 
         def quantise_w1(g):
             if not exists(g):
                 return
-            w1_codes[g] = ahead_pool.tile([P, K_PASS], U32, tag="w1_codes", name="w1_codes", align_bytes=64)
-            w1_scales[g] = ahead_pool.tile([P, K_PASS], U8, tag="w1_scales", name="w1_scales", align_bytes=64)
+            w1_codes[g] = ahead.tile([P, K_PASS], U32, tag="w1_codes", name="w1_codes", align_bytes=64)
+            w1_scales[g] = ahead.tile([P, K_PASS], U8, tag="w1_scales", name="w1_scales", align_bytes=64)
             nc.vector.quantize_mx(
                 out=w1_codes[g][:].bitcast(FP8X4), scales=w1_scales[g][:], in_=w1_grouped[g][:]
             )
@@ -199,29 +198,28 @@ def tile_waveletblock_k_kernel(tc, x, conv_w, conv_b, conv_out_w, conv_out_b, ou
                 out=w2_codes[:, g, :].bitcast(FP8X4), scales=w2_scales[:, g, :], in_=w2_grouped[g][:]
             )
 
-        def hidden_main(g, chunks):
+        def hidden_main(g, t):
             if not exists(g):
                 return
-            if g not in hidden:
-                hidden[g] = stage.tile([P, PACK, PIX], BF16, tag="hidden", name="hidden", bufs=3)
-            for t in chunks:
-                bank = work.tile([P, PIX_MAIN], F32, tag="work")
-                nc.tensor.matmul_mx(
-                    out=bank[:],
-                    lhsT=w1_codes[g][:, P * t : P * t + P].bitcast(FP8X4),
-                    lhsT_scale=w1_scales[g][:, P * t : P * t + P],
-                    rhs=d_codes[:, 0:PIX_MAIN].bitcast(FP8X4),
-                    rhs_scale=d_scales[:, 0:PIX_MAIN],
-                    start=True,
-                    stop=True,
-                )
-                nc.scalar.activation(
-                    out=hidden[g][:, t, 0:PIX_MAIN],
-                    in_=bank[:],
-                    func=FUNC.Silu,
-                    bias=hid_bias[:, PACK * g + t : PACK * g + t + 1],
-                    scale=1.0,
-                )
+            if t == 0:
+                hidden[g] = stage.tile([P, PACK, PIX], BF16, tag="hidden", name="hidden")
+            bank = work.tile([P, PIX_MAIN], F32, tag="work")
+            nc.tensor.matmul_mx(
+                out=bank[:],
+                lhsT=w1_codes[g][:, P * t : P * t + P].bitcast(FP8X4),
+                lhsT_scale=w1_scales[g][:, P * t : P * t + P],
+                rhs=d_codes[:, 0:PIX_MAIN].bitcast(FP8X4),
+                rhs_scale=d_scales[:, 0:PIX_MAIN],
+                start=True,
+                stop=True,
+            )
+            nc.scalar.activation(
+                out=hidden[g][:, t, 0:PIX_MAIN],
+                in_=bank[:],
+                func=FUNC.Silu,
+                bias=hid_bias[:, PACK * g + t : PACK * g + t + 1],
+                scale=1.0,
+            )
 
         def hidden_rest(g):
             if not exists(g):
@@ -249,8 +247,8 @@ def tile_waveletblock_k_kernel(tc, x, conv_w, conv_b, conv_out_w, conv_out_b, ou
         def regroup(g, first, last):
             if not exists(g):
                 return
-            if g not in f_grouped:
-                f_grouped[g] = stage.tile([P, PIX * PACK], BF16, tag="f_grouped", name="f_grouped", align_bytes=64)
+            if first == 0:
+                f_grouped[g] = stage.tile([P, PIX * PACK], BF16, tag="f_grouped", name="f_grouped", bufs=2, align_bytes=64)
             nc.vector.tensor_copy(
                 out=f_grouped[g][:, PACK * first : PACK * last].rearrange("p (c i t) -> p c t i", i=4, t=PACK),
                 in_=hidden[g][:, :, first:last].rearrange("p t (c i) -> p c t i", i=4),
@@ -259,8 +257,8 @@ def tile_waveletblock_k_kernel(tc, x, conv_w, conv_b, conv_out_w, conv_out_b, ou
         def quantise_main(g):
             if not exists(g):
                 return
-            f_codes[g] = stage.tile([P, PIX_MAIN], U32, tag="f_codes", name="f_codes", bufs=3, align_bytes=64)
-            f_scales[g] = stage.tile([P, PIX_MAIN], U8, tag="f_scales", name="f_scales", bufs=3, align_bytes=64)
+            f_codes[g] = stage.tile([P, PIX_MAIN], U32, tag="f_codes", name="f_codes", align_bytes=64)
+            f_scales[g] = stage.tile([P, PIX_MAIN], U8, tag="f_scales", name="f_scales", align_bytes=64)
             nc.vector.quantize_mx(
                 out=f_codes[g][:].bitcast(FP8X4),
                 scales=f_scales[g][:],
@@ -276,32 +274,36 @@ def tile_waveletblock_k_kernel(tc, x, conv_w, conv_b, conv_out_w, conv_out_b, ou
                 in_=f_grouped[g][:, PACK * PIX_MAIN : PACK * PIX],
             )
 
-        def output_main(g, subbands):
+        def output_main(g, s):
             if not exists(g):
                 return
-            for s in subbands:
-                nc.tensor.matmul_mx(
-                    out=y_main[s][:],
-                    lhsT=w2_codes[:, g, P * s : P * s + P].bitcast(FP8X4),
-                    lhsT_scale=w2_scales[:, g, P * s : P * s + P],
-                    rhs=f_codes[g][:].bitcast(FP8X4),
-                    rhs_scale=f_scales[g][:],
-                    start=(g == 0),
-                    stop=(g == GROUPS - 1),
-                )
+            nc.tensor.matmul_mx(
+                out=y_main[s][:],
+                lhsT=w2_codes[:, g, P * s : P * s + P].bitcast(FP8X4),
+                lhsT_scale=w2_scales[:, g, P * s : P * s + P],
+                rhs=f_codes[g][:].bitcast(FP8X4),
+                rhs_scale=f_scales[g][:],
+                start=(g == 0),
+                stop=(g == GROUPS - 1),
+            )
 
-        for step in range(-LEAD, GROUPS + 2):
+        for step in range(-LEAD, GROUPS + LAG):
             regroup(step - 1, 0, PIX_MAIN)
-            transpose_weights(step + LEAD)
-            quantise_main(step - 1)
-            hidden_main(step, (0, 1))
-            output_main(step - 2, (0, 1))
+            hidden_main(step, 0)
+            output_main(step - LAG, 0)
             regroup(step - 1, PIX_MAIN, PIX)
-            quantise_w1(step + LEAD)
+            transpose_w1(step + LEAD)
+            quantise_main(step - 1)
+            quantise_w2(step + LEAD - 1)
             quantise_rest(step - 1)
-            quantise_w2(step + LEAD)
-            hidden_main(step, (2, 3))
-            output_main(step - 2, (2, 3))
+            hidden_main(step, 1)
+            output_main(step - LAG, 1)
+            hidden_main(step, 2)
+            output_main(step - LAG, 2)
+            quantise_w1(step + LEAD)
+            hidden_main(step, 3)
+            output_main(step - LAG, 3)
+            transpose_w2(step + LEAD)
             hidden_rest(step)
 
         y_rest = work.tile([P, 4, FRAME_PIX], F32, tag="work")
@@ -325,9 +327,8 @@ def tile_waveletblock_k_kernel(tc, x, conv_w, conv_b, conv_out_w, conv_out_b, ou
         out_view = out.rearrange("b l c h w -> c (b l) (h w)")
         image_view = image[:].rearrange("c (l i) a w -> c l (i a w)", l=FRAMES)
 
-        def finish(first_frame, last_frame, banks):
+        def subband_pairs(first_frame, last_frame, banks):
             pix = slice(FRAME_PIX * first_frame, FRAME_PIX * last_frame)
-            lines = slice(16 * first_frame, 16 * last_frame)
             for s in (2, 3, 0, 1):
                 nc.scalar.activation(
                     out=z[:, s, pix],
@@ -339,18 +340,23 @@ def tile_waveletblock_k_kernel(tc, x, conv_w, conv_b, conv_out_w, conv_out_b, ou
             for pair, first in ((high, 2), (low, 0)):
                 nc.vector.tensor_sub(out=pair[:, 0, pix], in0=z[:, first, pix], in1=z[:, first + 1, pix])
                 nc.vector.tensor_add(out=pair[:, 1, pix], in0=z[:, first, pix], in1=z[:, first + 1, pix])
-            low_jb = low[:, :, pix].rearrange("c b (n j) -> c n j b", j=8)
-            high_jb = high[:, :, pix].rearrange("c b (n j) -> c n j b", j=8)
+
+        def rows_and_store(first_frame, last_frame):
+            pix = slice(FRAME_PIX * first_frame, FRAME_PIX * last_frame)
+            lines = slice(16 * first_frame, 16 * last_frame)
             for a, op in ((0, ALU.subtract), (1, ALU.add)):
                 nc.vector.tensor_tensor(
                     out=image[:, lines, a, :].rearrange("c n (j b) -> c n j b", b=2),
-                    in0=low_jb,
-                    in1=high_jb,
+                    in0=low[:, :, pix].rearrange("c b (n j) -> c n j b", j=8),
+                    in1=high[:, :, pix].rearrange("c b (n j) -> c n j b", j=8),
                     op=op,
                 )
             nc.sync.dma_start(
                 out=out_view[:, first_frame:last_frame, :], in_=image_view[:, first_frame:last_frame, :]
             )
 
-        finish(0, 4, [y_main[s][:] for s in range(4)])
-        finish(4, 5, [y_rest[:, s, :] for s in range(4)])
+        subband_pairs(0, 4, [y_main[s][:] for s in range(4)])
+        rows_and_store(0, 2)
+        rows_and_store(2, 4)
+        subband_pairs(4, 5, [y_rest[:, s, :] for s in range(4)])
+        rows_and_store(4, 5)

@@ -169,7 +169,9 @@ def tile_waveletblock_k_kernel(tc, x, conv_w, conv_b, conv_out_w, conv_out_b, ou
             w1_grouped[g] = ahead.tile([P, K_PASS * PACK], BF16, tag="w1_grouped", name="w1_grouped", align_bytes=64)
             words = w1_words[g]
             transpose_512_columns(
-                lambda half, u, e: words[:, half, 256 * e + P * u : 256 * e + P * u + P], w1_grouped[g], g >= LEAD
+                lambda half, u, e: words[:, half, 256 * e + P * u : 256 * e + P * u + P],
+                w1_grouped[g],
+                g >= LEAD and g % 2 == 1,
             )
 
         def transpose_w2(g):

@@ -21,9 +21,7 @@ PIX_MAIN = 4 * FRAME_PIX
 WAVE = 512
 HID = 8192
 GROUPS = HID // K_PASS
-RAW_BUFS = 6
-LEAD = 3
-LAG = 2
+RAW_BUFS = 8
 
 FLOPS = 2 * 2 * HID * WAVE * PIX
 
@@ -34,8 +32,8 @@ def tile_waveletblock_k_kernel(tc, x, conv_w, conv_b, conv_out_w, conv_out_b, ou
         ctx.enter_context(tc.manual_schedule())
         keep = ctx.enter_context(tc.tile_pool(name="keep", bufs=1))
         raw = ctx.enter_context(tc.tile_pool(name="raw", bufs=RAW_BUFS))
-        ahead = ctx.enter_context(tc.tile_pool(name="ahead", bufs=LEAD + 1))
-        stage = ctx.enter_context(tc.tile_pool(name="stage", bufs=LAG + 1))
+        ahead = ctx.enter_context(tc.tile_pool(name="ahead", bufs=4))
+        stage = ctx.enter_context(tc.tile_pool(name="stage", bufs=2))
         acc = ctx.enter_context(tc.psum_pool(name="acc", bufs=1))
         work = ctx.enter_context(tc.psum_pool(name="work", bufs=4))
 
@@ -55,38 +53,57 @@ def tile_waveletblock_k_kernel(tc, x, conv_w, conv_b, conv_out_w, conv_out_b, ou
         nc.sync.dma_start(out=out_bias_rows[0:4, :], in_=conv_out_b.rearrange("(s c) -> s c", c=P))
         x_view = x.rearrange("b l (q e) h w -> q (b l) (e h w)", e=2)
         x_sb = keep.tile([P, FRAMES, 2 * 512], BF16)
-        for frame in range(FRAMES):
-            nc.sync.dma_start(out=x_sb[0:64, frame, :], in_=x_view[:, frame, :])
-            nc.scalar.dma_start(out=x_sb[64:128, frame, :], in_=x_view[:, frame, :])
+        for first, last in ((0, 2), (2, FRAMES)):
+            nc.sync.dma_start(out=x_sb[0:64, first:last, :], in_=x_view[:, first:last, :])
+            nc.scalar.dma_start(out=x_sb[64:128, first:last, 0 : 2 * 512 - 16], in_=x_view[:, first:last, 16:])
 
         w1_view = conv_w.rearrange("(g u j e) k -> g j u (e k)", u=2, j=P, e=2)
         w2_view = conv_out_w.rearrange("(s m) (g o) -> g m s o", m=P, o=K_PASS)
         w1_words = {}
         w2_words = {}
 
-        def load_weights(g):
-            if g >= GROUPS:
-                return
-            w1_raw = raw.tile([P, 2, 2 * WAVE], BF16, tag="w1_raw")
-            nc.sync.dma_start(out=w1_raw[:], in_=w1_view[g])
-            w2_raw = raw.tile([P, 4, K_PASS], BF16, tag="w2_raw")
-            nc.sync.dma_start(out=w2_raw[:], in_=w2_view[g])
-            w1_words[g] = w1_raw[:].bitcast(F32)
-            w2_words[g] = w2_raw[:].bitcast(F32)
+        def exists(g):
+            return 0 <= g < GROUPS
 
+        def load_w1(g):
+            if exists(g):
+                w1_raw = raw.tile([P, 2, 2 * WAVE], BF16, tag="w1_raw")
+                nc.sync.dma_start(out=w1_raw[:], in_=w1_view[g])
+                w1_words[g] = w1_raw[:].bitcast(F32)
+
+        def load_w2(g):
+            if exists(g):
+                w2_raw = raw.tile([P, 4, K_PASS], BF16, tag="w2_raw")
+                nc.sync.dma_start(out=w2_raw[:], in_=w2_view[g])
+                w2_words[g] = w2_raw[:].bitcast(F32)
+
+        load_w1(0)
         for g in range(RAW_BUFS):
-            load_weights(g)
+            if g + 1 < RAW_BUFS:
+                load_w1(g + 1)
+            load_w2(g)
 
         ident = keep.tile([P, P], F32)
         make_identity(nc, ident[:])
-        sign = keep.tile([P, 1], F32)
-        nc.vector.memset(sign[0:64], 1.0)
-        nc.vector.memset(sign[64:128], -1.0)
+        row_sign = keep.tile([P, 1], F32)
+        nc.vector.memset(row_sign[0:64], -1.0)
+        nc.vector.memset(row_sign[64:128], 1.0)
         zero = keep.tile([P, 1], F32)
         nc.vector.memset(zero[:], 0.0)
         warm = keep.tile([P, 1], F32)
         nc.scalar.activation(out=warm[:], in_=zero[:], func=FUNC.Silu)
 
+        pairs64 = keep.tile([P, 2, 64], F32)
+        haar = keep.tile([P, 2, 192], BF16)
+        for copy in range(2):
+            nc.vector.tensor_add(out=pairs64[:, copy, :], in0=ident[:, 0:64], in1=ident[:, 64:128])
+        pairs_flat = pairs64[:].rearrange("p r c -> p (r c)")
+        for cols, factor in ((slice(0, 128), 0.5), (slice(128, 192), -0.5)):
+            src = pairs_flat[:, 0 : cols.stop - cols.start]
+            nc.vector.tensor_scalar_mul(out=haar[:, 0, cols], in0=src, scalar1=factor)
+            nc.vector.tensor_scalar(
+                out=haar[:, 1, cols], in0=src, scalar1=row_sign[:, 0:1], scalar2=factor, op0=ALU.mult, op1=ALU.mult
+            )
         bias_f32 = keep.tile([P, 3, P], F32)
         nc.vector.tensor_copy(
             out=bias_f32[:, 0:2, :], in_=hid_bias_rows[:].rearrange("r (j e) -> r e j", e=2)
@@ -98,56 +115,50 @@ def tile_waveletblock_k_kernel(tc, x, conv_w, conv_b, conv_out_w, conv_out_b, ou
 
         hid_bias = keep.tile([P, PACK * GROUPS], F32)
         out_bias_half = keep.tile([P, 4], F32)
-        with tc.tile_pool(name="head", bufs=1) as head:
-            col_step = head.tile([P, FRAMES, 2 * 256], F32)
-            for frame in range(FRAMES):
-                x_cols = x_sb[:, frame, :].rearrange("p (n b) -> p n b", b=2)
-                nc.vector.scalar_tensor_tensor(
-                    out=col_step[:, frame, :],
-                    in0=x_cols[:, :, 0],
-                    scalar=sign[:, 0:1],
-                    in1=x_cols[:, :, 1],
-                    op0=ALU.mult,
-                    op1=ALU.add,
-                )
-            nc.vector.tensor_copy(
-                out=hid_bias[:].rearrange("j (r e) -> j r e", e=2),
-                in_=bias_bank[:, 0:2, 0 : 2 * GROUPS].rearrange("j e r -> j r e"),
+        row_bias = keep.tile([P, 2], F32)
+        nc.vector.tensor_copy(
+            out=hid_bias[:].rearrange("j (r e) -> j r e", e=2),
+            in_=bias_bank[:, 0:2, 0 : 2 * GROUPS].rearrange("j e r -> j r e"),
+        )
+        nc.vector.tensor_scalar_mul(out=out_bias_half[:], in0=bias_bank[:, 2, 0:4], scalar1=0.5)
+        nc.vector.tensor_sub(out=row_bias[:, 0:1], in0=out_bias_half[:, 0:1], in1=out_bias_half[:, 2:3])
+        nc.vector.tensor_add(out=row_bias[:, 1:2], in0=out_bias_half[:, 0:1], in1=out_bias_half[:, 2:3])
+
+        for frame in range(FRAMES):
+            bank = work.tile([P, PACK, FRAME_PIX], F32, tag="work")
+            for u in range(2):
+                for e in range(2):
+                    x_even_rows = x_sb[:, frame, 512 * e : 512 * e + 512].rearrange(
+                        "p (i a j b) -> p i a j b", a=2, j=8, b=2
+                    )
+                    for b in range(2):
+                        nc.tensor.matmul(
+                            out=bank[:, 2 * u + e, :].rearrange("p (i j) -> p i j", j=8),
+                            lhsT=haar[:, u, 64 * (1 - b) : 64 * (1 - b) + P],
+                            rhs=x_even_rows[:, :, 0, :, b],
+                            start=(b == 0),
+                            stop=(b == 1),
+                        )
+            dst = d_grouped[:, PACK * FRAME_PIX * frame : PACK * FRAME_PIX * (frame + 1)].rearrange(
+                "p (n t) -> p n t", t=PACK
             )
-            nc.vector.tensor_scalar_mul(out=out_bias_half[:], in0=bias_bank[:, 2, 0:4], scalar1=0.5)
-            rows = col_step[:].rearrange("p l (e i a j) -> p l e i a j", e=2, i=16, a=2)
-            twice_d = head.tile([P, 2, 2, FRAMES, FRAME_PIX], F32)
-            for u, op in ((0, ALU.add), (1, ALU.subtract)):
-                nc.vector.tensor_tensor(
-                    out=twice_d[:, u].rearrange("p e l (i j) -> p l e i j", j=8),
-                    in0=rows[:, :, :, :, 1, :],
-                    in1=rows[:, :, :, :, 0, :],
-                    op=op,
-                )
-            nc.vector.tensor_scalar_mul(
-                out=d_grouped[:].rearrange("p (n t) -> p n t", t=PACK),
-                in0=twice_d[:].rearrange("p u e l n -> p (l n) (u e)"),
-                scalar1=0.5,
-            )
-        for first, last in ((0, PIX_MAIN), (PIX_MAIN, PIX)):
-            nc.vector.quantize_mx(
-                out=d_codes[:, first:last].bitcast(FP8X4),
-                scales=d_scales[:, first:last],
-                in_=d_grouped[:, PACK * first : PACK * last],
-            )
+            src = bank[:].rearrange("p t n -> p n t")
+            if frame % 2 == 0:
+                nc.vector.tensor_copy(out=dst, in_=src)
+            else:
+                nc.scalar.copy(out=dst, in_=src)
 
         w1_grouped = {}
         w2_grouped = {}
         w1_codes = {}
         w1_scales = {}
         hidden = {}
+        hidden_r = {}
         f_grouped = {}
+        fr_grouped = {}
         f_codes = {}
         f_scales = {}
         y_main = [acc.tile([P, PIX_MAIN], F32, name="y_main%d" % s) for s in range(4)]
-
-        def exists(g):
-            return 0 <= g < GROUPS
 
         def transpose_512_columns(block, grouped, vector_helps):
             pairs = grouped[:].bitcast(F32).rearrange("p (c u) -> p c u", u=2)
@@ -166,23 +177,24 @@ def tile_waveletblock_k_kernel(tc, x, conv_w, conv_b, conv_out_w, conv_out_b, ou
         def transpose_w1(g):
             if not exists(g):
                 return
-            w1_grouped[g] = ahead.tile([P, K_PASS * PACK], BF16, tag="w1_grouped", name="w1_grouped", align_bytes=64)
+            w1_grouped[g] = ahead.tile([P, K_PASS * PACK], BF16, tag="w1_grouped", name="w1_grouped", bufs=2, align_bytes=64)
             words = w1_words[g]
             transpose_512_columns(
                 lambda half, u, e: words[:, half, 256 * e + P * u : 256 * e + P * u + P],
                 w1_grouped[g],
-                g >= LEAD and g % 2 == 1,
+                g % 2 == 1,
             )
+            load_w1(g + RAW_BUFS)
 
         def transpose_w2(g):
             if not exists(g):
                 return
-            w2_grouped[g] = ahead.tile([P, K_PASS * PACK], BF16, tag="w2_grouped", name="w2_grouped", align_bytes=64)
+            w2_grouped[g] = ahead.tile([P, K_PASS * PACK], BF16, tag="w2_grouped", name="w2_grouped", bufs=2, align_bytes=64)
             words = w2_words[g]
             transpose_512_columns(
-                lambda half, u, s: words[:, 2 * half + s, P * u : P * u + P], w2_grouped[g], g >= LEAD
+                lambda half, u, s: words[:, 2 * half + s, P * u : P * u + P], w2_grouped[g], True
             )
-            load_weights(g + RAW_BUFS)
+            load_w2(g + RAW_BUFS)
 
         def quantise_w1(g):
             if not exists(g):
@@ -204,7 +216,7 @@ def tile_waveletblock_k_kernel(tc, x, conv_w, conv_b, conv_out_w, conv_out_b, ou
             if not exists(g):
                 return
             if t == 0:
-                hidden[g] = stage.tile([P, PACK, PIX], BF16, tag="hidden", name="hidden")
+                hidden[g] = stage.tile([P, PACK, PIX_MAIN], BF16, tag="hidden", name="hidden")
             bank = work.tile([P, PIX_MAIN], F32, tag="work")
             nc.tensor.matmul_mx(
                 out=bank[:],
@@ -216,7 +228,7 @@ def tile_waveletblock_k_kernel(tc, x, conv_w, conv_b, conv_out_w, conv_out_b, ou
                 stop=True,
             )
             nc.scalar.activation(
-                out=hidden[g][:, t, 0:PIX_MAIN],
+                out=hidden[g][:, t, :],
                 in_=bank[:],
                 func=FUNC.Silu,
                 bias=hid_bias[:, PACK * g + t : PACK * g + t + 1],
@@ -226,6 +238,7 @@ def tile_waveletblock_k_kernel(tc, x, conv_w, conv_b, conv_out_w, conv_out_b, ou
         def hidden_rest(g):
             if not exists(g):
                 return
+            hidden_r[g] = stage.tile([P, PACK, FRAME_PIX], BF16, tag="hidden_r", name="hidden_r")
             bank = work.tile([P, PACK, FRAME_PIX], F32, tag="work")
             for t in range(PACK):
                 nc.tensor.matmul_mx(
@@ -239,32 +252,40 @@ def tile_waveletblock_k_kernel(tc, x, conv_w, conv_b, conv_out_w, conv_out_b, ou
                 )
             for t in range(PACK):
                 nc.scalar.activation(
-                    out=hidden[g][:, t, PIX_MAIN:PIX],
+                    out=hidden_r[g][:, t, :],
                     in_=bank[:, t, :],
                     func=FUNC.Silu,
                     bias=hid_bias[:, PACK * g + t : PACK * g + t + 1],
                     scale=1.0,
                 )
 
-        def regroup(g, first, last):
+        def regroup(dst, src):
+            nc.vector.tensor_copy(
+                out=dst[:].rearrange("p (c i t) -> p c t i", i=4, t=PACK),
+                in_=src[:].rearrange("p t (c i) -> p c t i", i=4),
+            )
+
+        def regroup_main(g):
             if not exists(g):
                 return
-            if first == 0:
-                f_grouped[g] = stage.tile([P, PIX * PACK], BF16, tag="f_grouped", name="f_grouped", bufs=2, align_bytes=64)
-            nc.vector.tensor_copy(
-                out=f_grouped[g][:, PACK * first : PACK * last].rearrange("p (c i t) -> p c t i", i=4, t=PACK),
-                in_=hidden[g][:, :, first:last].rearrange("p t (c i) -> p c t i", i=4),
-            )
+            f_grouped[g] = stage.tile([P, PIX_MAIN * PACK], BF16, tag="f_grouped", name="f_grouped", align_bytes=64)
+            regroup(f_grouped[g], hidden[g])
+
+        def regroup_rest(g):
+            if not exists(g):
+                return
+            fr_grouped[g] = stage.tile([P, FRAME_PIX * PACK], BF16, tag="fr_grouped", name="fr_grouped", align_bytes=64)
+            regroup(fr_grouped[g], hidden_r[g])
 
         def quantise_main(g):
             if not exists(g):
                 return
-            f_codes[g] = stage.tile([P, PIX_MAIN], U32, tag="f_codes", name="f_codes", align_bytes=64)
-            f_scales[g] = stage.tile([P, PIX_MAIN], U8, tag="f_scales", name="f_scales", align_bytes=64)
+            f_codes[g] = stage.tile([P, PIX_MAIN], U32, tag="f_codes", name="f_codes", bufs=3, align_bytes=64)
+            f_scales[g] = stage.tile([P, PIX_MAIN], U8, tag="f_scales", name="f_scales", bufs=3, align_bytes=64)
             nc.vector.quantize_mx(
                 out=f_codes[g][:].bitcast(FP8X4),
                 scales=f_scales[g][:],
-                in_=f_grouped[g][:, 0 : PACK * PIX_MAIN],
+                in_=f_grouped[g][:],
             )
 
         def quantise_rest(g):
@@ -273,7 +294,7 @@ def tile_waveletblock_k_kernel(tc, x, conv_w, conv_b, conv_out_w, conv_out_b, ou
             nc.vector.quantize_mx(
                 out=rest_codes[:, g, :].bitcast(FP8X4),
                 scales=rest_scales[:, g, :],
-                in_=f_grouped[g][:, PACK * PIX_MAIN : PACK * PIX],
+                in_=fr_grouped[g][:],
             )
 
         def output_main(g, s):
@@ -289,24 +310,36 @@ def tile_waveletblock_k_kernel(tc, x, conv_w, conv_b, conv_out_w, conv_out_b, ou
                 stop=(g == GROUPS - 1),
             )
 
-        for step in range(-LEAD, GROUPS + LAG):
-            regroup(step - 1, 0, PIX_MAIN)
+        transpose_w1(0)
+        for first, last in ((0, PIX_MAIN), (PIX_MAIN, PIX)):
+            nc.vector.quantize_mx(
+                out=d_codes[:, first:last].bitcast(FP8X4),
+                scales=d_scales[:, first:last],
+                in_=d_grouped[:, PACK * first : PACK * last],
+            )
+        quantise_w1(0)
+        transpose_w1(1)
+        transpose_w2(0)
+        quantise_w1(1)
+
+        for step in range(GROUPS + 2):
+            regroup_main(step - 1)
             hidden_main(step, 0)
-            output_main(step - LAG, 0)
-            regroup(step - 1, PIX_MAIN, PIX)
-            transpose_w1(step + LEAD)
+            output_main(step - 2, 1)
+            regroup_rest(step - 2)
+            transpose_w1(step + 2)
             quantise_main(step - 1)
-            quantise_w2(step + LEAD - 1)
-            quantise_rest(step - 1)
+            quantise_w2(step)
+            quantise_rest(step - 2)
             hidden_main(step, 1)
-            output_main(step - LAG, 1)
+            output_main(step - 2, 0)
             hidden_main(step, 2)
-            output_main(step - LAG, 2)
-            quantise_w1(step + LEAD)
+            output_main(step - 2, 3)
+            quantise_w1(step + 2)
             hidden_main(step, 3)
-            output_main(step - LAG, 3)
-            transpose_w2(step + LEAD)
-            hidden_rest(step)
+            output_main(step - 2, 2)
+            transpose_w2(step + 1)
+            hidden_rest(step - 1)
 
         y_rest = work.tile([P, 4, FRAME_PIX], F32, tag="work")
         for s in range(4):
@@ -322,7 +355,7 @@ def tile_waveletblock_k_kernel(tc, x, conv_w, conv_b, conv_out_w, conv_out_b, ou
                 )
 
         tail = ctx.enter_context(tc.tile_pool(name="tail", bufs=1))
-        z = tail.tile([P, 4, PIX], F32)
+        z = tail.tile([P, 2, PIX], F32)
         low = tail.tile([P, 2, PIX], F32)
         high = tail.tile([P, 2, PIX], F32)
         image = tail.tile([P, FRAMES * 16, 2, 16], F32)
@@ -331,27 +364,30 @@ def tile_waveletblock_k_kernel(tc, x, conv_w, conv_b, conv_out_w, conv_out_b, ou
 
         def subband_pairs(first_frame, last_frame, banks):
             pix = slice(FRAME_PIX * first_frame, FRAME_PIX * last_frame)
-            for s in (2, 3, 0, 1):
+            for r, pair in ((0, low), (1, high)):
                 nc.scalar.activation(
-                    out=z[:, s, pix],
-                    in_=banks[s],
+                    out=z[:, r, pix],
+                    in_=banks[2 * r + 1],
                     func=FUNC.Identity,
-                    bias=out_bias_half[:, s : s + 1],
+                    bias=out_bias_half[:, 2 * r + 1 : 2 * r + 2],
                     scale=0.5,
                 )
-            for pair, first in ((high, 2), (low, 0)):
-                nc.vector.tensor_sub(out=pair[:, 0, pix], in0=z[:, first, pix], in1=z[:, first + 1, pix])
-                nc.vector.tensor_add(out=pair[:, 1, pix], in0=z[:, first, pix], in1=z[:, first + 1, pix])
+                for b, op in ((0, ALU.subtract), (1, ALU.add)):
+                    nc.vector.scalar_tensor_tensor(
+                        out=pair[:, b, pix], in0=banks[2 * r], scalar=0.5, in1=z[:, r, pix], op0=ALU.mult, op1=op
+                    )
 
         def rows_and_store(first_frame, last_frame):
             pix = slice(FRAME_PIX * first_frame, FRAME_PIX * last_frame)
             lines = slice(16 * first_frame, 16 * last_frame)
             for a, op in ((0, ALU.subtract), (1, ALU.add)):
-                nc.vector.tensor_tensor(
+                nc.vector.scalar_tensor_tensor(
                     out=image[:, lines, a, :].rearrange("c n (j b) -> c n j b", b=2),
                     in0=low[:, :, pix].rearrange("c b (n j) -> c n j b", j=8),
+                    scalar=row_bias[:, a : a + 1],
                     in1=high[:, :, pix].rearrange("c b (n j) -> c n j b", j=8),
-                    op=op,
+                    op0=ALU.add,
+                    op1=op,
                 )
             nc.sync.dma_start(
                 out=out_view[:, first_frame:last_frame, :], in_=image_view[:, first_frame:last_frame, :]

@@ -261,8 +261,8 @@ def tile_waveletblock_k_kernel(tc, x, conv_w, conv_b, conv_out_w, conv_out_b, ou
 
         def regroup(dst, src):
             nc.vector.tensor_copy(
-                out=dst[:].rearrange("p (c i t) -> p c t i", i=4, t=PACK),
-                in_=src[:].rearrange("p t (c i) -> p c t i", i=4),
+                out=dst[:].rearrange("p (c i t) -> p c t i", i=8, t=PACK),
+                in_=src[:].rearrange("p t (c i) -> p c t i", i=8),
             )
 
         def regroup_main(g):

@@ -182,7 +182,7 @@ def tile_waveletblock_k_kernel(tc, x, conv_w, conv_b, conv_out_w, conv_out_b, ou
             transpose_512_columns(
                 lambda half, u, e: words[:, half, 256 * e + P * u : 256 * e + P * u + P],
                 w1_grouped[g],
-                g % 2 == 1,
+                g % 2 == 0,
             )
             load_w1(g + RAW_BUFS)
 
@@ -216,7 +216,7 @@ def tile_waveletblock_k_kernel(tc, x, conv_w, conv_b, conv_out_w, conv_out_b, ou
             if not exists(g):
                 return
             if t == 0:
-                hidden[g] = stage.tile([P, PACK, PIX_MAIN], BF16, tag="hidden", name="hidden")
+                hidden[g] = stage.tile([P, PIX_MAIN // 8, PACK, 8], BF16, tag="hidden", name="hidden")
             bank = work.tile([P, PIX_MAIN], F32, tag="work")
             nc.tensor.matmul_mx(
                 out=bank[:],
@@ -228,8 +228,8 @@ def tile_waveletblock_k_kernel(tc, x, conv_w, conv_b, conv_out_w, conv_out_b, ou
                 stop=True,
             )
             nc.scalar.activation(
-                out=hidden[g][:, t, :],
-                in_=bank[:],
+                out=hidden[g][:, :, t, :],
+                in_=bank[:].rearrange("p (c i) -> p c i", i=8),
                 func=FUNC.Silu,
                 bias=hid_bias[:, PACK * g + t : PACK * g + t + 1],
                 scale=1.0,
@@ -238,7 +238,7 @@ def tile_waveletblock_k_kernel(tc, x, conv_w, conv_b, conv_out_w, conv_out_b, ou
         def hidden_rest(g):
             if not exists(g):
                 return
-            hidden_r[g] = stage.tile([P, PACK, FRAME_PIX], BF16, tag="hidden_r", name="hidden_r")
+            hidden_r[g] = stage.tile([P, FRAME_PIX // 8, PACK, 8], BF16, tag="hidden_r", name="hidden_r")
             bank = work.tile([P, PACK, FRAME_PIX], F32, tag="work")
             for t in range(PACK):
                 nc.tensor.matmul_mx(
@@ -252,8 +252,8 @@ def tile_waveletblock_k_kernel(tc, x, conv_w, conv_b, conv_out_w, conv_out_b, ou
                 )
             for t in range(PACK):
                 nc.scalar.activation(
-                    out=hidden_r[g][:, t, :],
-                    in_=bank[:, t, :],
+                    out=hidden_r[g][:, :, t, :],
+                    in_=bank[:, t, :].rearrange("p (c i) -> p c i", i=8),
                     func=FUNC.Silu,
                     bias=hid_bias[:, PACK * g + t : PACK * g + t + 1],
                     scale=1.0,
@@ -262,7 +262,7 @@ def tile_waveletblock_k_kernel(tc, x, conv_w, conv_b, conv_out_w, conv_out_b, ou
         def regroup(dst, src):
             nc.vector.tensor_copy(
                 out=dst[:].rearrange("p (c i t) -> p c t i", i=8, t=PACK),
-                in_=src[:].rearrange("p t (c i) -> p c t i", i=8),
+                in_=src[:],
             )
 
         def regroup_main(g):

@@ -238,7 +238,7 @@ def tile_waveletblock_k_kernel(tc, x, conv_w, conv_b, conv_out_w, conv_out_b, ou
         def hidden_rest(g):
             if not exists(g):
                 return
-            hidden_r[g] = stage.tile([P, FRAME_PIX // 8, PACK, 8], BF16, tag="hidden_r", name="hidden_r")
+            hidden_r[g] = stage.tile([P, FRAME_PIX // 8, PACK, 8], BF16, tag="hidden_r", name="hidden_r", bufs=3)
             bank = work.tile([P, PACK, FRAME_PIX], F32, tag="work")
             for t in range(PACK):
                 nc.tensor.matmul_mx(
@@ -259,33 +259,33 @@ def tile_waveletblock_k_kernel(tc, x, conv_w, conv_b, conv_out_w, conv_out_b, ou
                     scale=1.0,
                 )
 
-        def regroup(dst, src):
-            nc.vector.tensor_copy(
-                out=dst[:].rearrange("p (c i t) -> p c t i", i=8, t=PACK),
-                in_=src[:],
-            )
+        def regroup(copy, dst, src):
+            copy(out=dst.rearrange("p (c i t) -> p c t i", i=8, t=PACK), in_=src)
+
+        def main_tiles(g):
+            f_grouped[g] = stage.tile([P, PIX_MAIN * PACK], BF16, tag="f_grouped", name="f_grouped", align_bytes=64)
+            f_codes[g] = stage.tile([P, PIX_MAIN], U32, tag="f_codes", name="f_codes", bufs=3, align_bytes=64)
+            f_scales[g] = stage.tile([P, PIX_MAIN], U8, tag="f_scales", name="f_scales", bufs=3, align_bytes=64)
 
         def regroup_main(g):
             if not exists(g):
                 return
-            f_grouped[g] = stage.tile([P, PIX_MAIN * PACK], BF16, tag="f_grouped", name="f_grouped", align_bytes=64)
-            regroup(f_grouped[g], hidden[g])
+            main_tiles(g)
+            regroup(nc.vector.tensor_copy, f_grouped[g][:], hidden[g][:])
 
         def regroup_rest(g):
             if not exists(g):
                 return
             fr_grouped[g] = stage.tile([P, FRAME_PIX * PACK], BF16, tag="fr_grouped", name="fr_grouped", align_bytes=64)
-            regroup(fr_grouped[g], hidden_r[g])
+            regroup(nc.vector.tensor_copy, fr_grouped[g][:], hidden_r[g][:])
 
-        def quantise_main(g):
+        def quantise_main(g, first=0, last=PIX_MAIN):
             if not exists(g):
                 return
-            f_codes[g] = stage.tile([P, PIX_MAIN], U32, tag="f_codes", name="f_codes", bufs=3, align_bytes=64)
-            f_scales[g] = stage.tile([P, PIX_MAIN], U8, tag="f_scales", name="f_scales", bufs=3, align_bytes=64)
             nc.vector.quantize_mx(
-                out=f_codes[g][:].bitcast(FP8X4),
-                scales=f_scales[g][:],
-                in_=f_grouped[g][:],
+                out=f_codes[g][:, first:last].bitcast(FP8X4),
+                scales=f_scales[g][:, first:last],
+                in_=f_grouped[g][:, PACK * first : PACK * last],
             )
 
         def quantise_rest(g):
@@ -297,15 +297,15 @@ def tile_waveletblock_k_kernel(tc, x, conv_w, conv_b, conv_out_w, conv_out_b, ou
                 in_=fr_grouped[g][:],
             )
 
-        def output_main(g, s):
+        def output_main(g, s, first=0, last=PIX_MAIN):
             if not exists(g):
                 return
             nc.tensor.matmul_mx(
-                out=y_main[s][:],
+                out=y_main[s][:, first:last],
                 lhsT=w2_codes[:, g, P * s : P * s + P].bitcast(FP8X4),
                 lhsT_scale=w2_scales[:, g, P * s : P * s + P],
-                rhs=f_codes[g][:].bitcast(FP8X4),
-                rhs_scale=f_scales[g][:],
+                rhs=f_codes[g][:, first:last].bitcast(FP8X4),
+                rhs_scale=f_scales[g][:, first:last],
                 start=(g == 0),
                 stop=(g == GROUPS - 1),
             )
@@ -322,7 +322,7 @@ def tile_waveletblock_k_kernel(tc, x, conv_w, conv_b, conv_out_w, conv_out_b, ou
         transpose_w2(0)
         quantise_w1(1)
 
-        for step in range(GROUPS + 2):
+        for step in range(GROUPS - 1):
             regroup_main(step - 1)
             hidden_main(step, 0)
             output_main(step - 2, 1)
@@ -340,19 +340,6 @@ def tile_waveletblock_k_kernel(tc, x, conv_w, conv_b, conv_out_w, conv_out_b, ou
             output_main(step - 2, 2)
             transpose_w2(step + 1)
             hidden_rest(step - 1)
-
-        y_rest = work.tile([P, 4, FRAME_PIX], F32, tag="work")
-        for s in range(4):
-            for g in range(GROUPS):
-                nc.tensor.matmul_mx(
-                    out=y_rest[:, s, :],
-                    lhsT=w2_codes[:, g, P * s : P * s + P].bitcast(FP8X4),
-                    lhsT_scale=w2_scales[:, g, P * s : P * s + P],
-                    rhs=rest_codes[:, g, :].bitcast(FP8X4),
-                    rhs_scale=rest_scales[:, g, :],
-                    start=(g == 0),
-                    stop=(g == GROUPS - 1),
-                )
 
         tail = ctx.enter_context(tc.tile_pool(name="tail", bufs=1))
         z = tail.tile([P, 2, PIX], F32)
@@ -393,8 +380,60 @@ def tile_waveletblock_k_kernel(tc, x, conv_w, conv_b, conv_out_w, conv_out_b, ou
                 out=out_view[:, first_frame:last_frame, :], in_=image_view[:, first_frame:last_frame, :]
             )
 
+        LAST = GROUPS - 1
+        HALF = PIX_MAIN // 2
+        ORDER = (1, 0, 3, 2)
+        y_rest = {}
+
+        def output_rest(s, groups):
+            if s not in y_rest:
+                y_rest[s] = work.tile([P, FRAME_PIX], F32, tag="work", name="y_rest")
+            for g in groups:
+                nc.tensor.matmul_mx(
+                    out=y_rest[s][:],
+                    lhsT=w2_codes[:, g, P * s : P * s + P].bitcast(FP8X4),
+                    lhsT_scale=w2_scales[:, g, P * s : P * s + P],
+                    rhs=rest_codes[:, g, :].bitcast(FP8X4),
+                    rhs_scale=rest_scales[:, g, :],
+                    start=(g == 0),
+                    stop=(g == LAST),
+                )
+
+        regroup_main(LAST - 1)
+        hidden_main(LAST, 0)
+        output_main(LAST - 2, 1)
+        quantise_main(LAST - 1)
+        quantise_w2(LAST)
+        hidden_main(LAST, 1)
+        output_main(LAST - 2, 0)
+        hidden_main(LAST, 2)
+        output_main(LAST - 2, 3)
+        hidden_main(LAST, 3)
+        output_main(LAST - 2, 2)
+        main_tiles(LAST)
+        blocks = HALF // 8
+        regroup(nc.vector.tensor_copy, f_grouped[LAST][:, 0 : PACK * HALF], hidden[LAST][:, 0:blocks])
+        regroup(nc.scalar.copy, f_grouped[LAST][:, PACK * HALF :], hidden[LAST][:, blocks:])
+        hidden_rest(LAST - 1)
+        hidden_rest(LAST)
+        for s in ORDER:
+            output_main(LAST - 1, s)
+        regroup_rest(LAST - 2)
+        quantise_main(LAST, 0, HALF)
+        quantise_main(LAST, HALF, PIX_MAIN)
+        quantise_rest(LAST - 2)
+        for s in ORDER:
+            output_main(LAST, s)
+        regroup_rest(LAST - 1)
+        regroup_rest(LAST)
+        quantise_rest(LAST - 1)
+        quantise_rest(LAST)
         subband_pairs(0, 4, [y_main[s][:] for s in range(4)])
+        for s in ORDER:
+            output_rest(s, range(LAST - 1))
+        for s in ORDER:
+            output_rest(s, range(LAST - 1, GROUPS))
         rows_and_store(0, 2)
         rows_and_store(2, 4)
-        subband_pairs(4, 5, [y_rest[:, s, :] for s in range(4)])
+        subband_pairs(4, 5, [y_rest[s][:] for s in range(4)])
         rows_and_store(4, 5)

from contextlib import ExitStack

import concourse.mybir as mybir
from concourse.masks import make_identity

F32 = mybir.dt.float32
BF16 = mybir.dt.bfloat16
U32 = mybir.dt.uint32
U8 = mybir.dt.uint8
FP8X4 = mybir.dt.float8_e4m3fn_x4
ALU = mybir.AluOpType
FUNC = mybir.ActivationFunctionType

P = 128
PACK = 4
K_PASS = P * PACK
FRAMES = 5
FRAME_PIX = 128
PIX = FRAMES * FRAME_PIX
PIX_MAIN = 4 * FRAME_PIX
WAVE = 512
HID = 8192
GROUPS = HID // K_PASS
RAW_BUFS = 8

FLOPS = 2 * 2 * HID * WAVE * PIX


def tile_waveletblock_k_kernel(tc, x, conv_w, conv_b, conv_out_w, conv_out_b, out):
    nc = tc.nc
    with ExitStack() as ctx:
        ctx.enter_context(tc.manual_schedule())
        keep = ctx.enter_context(tc.tile_pool(name="keep", bufs=1))
        raw = ctx.enter_context(tc.tile_pool(name="raw", bufs=RAW_BUFS))
        ahead = ctx.enter_context(tc.tile_pool(name="ahead", bufs=4))
        stage = ctx.enter_context(tc.tile_pool(name="stage", bufs=2))
        acc = ctx.enter_context(tc.psum_pool(name="acc", bufs=1))
        work = ctx.enter_context(tc.psum_pool(name="work", bufs=4))

        d_grouped = keep.tile([P, PIX * PACK], BF16, align_bytes=64)
        d_codes = keep.tile([P, PIX], U32, align_bytes=64)
        d_scales = keep.tile([P, PIX], U8, align_bytes=64)
        w2_codes = keep.tile([P, GROUPS, K_PASS], U32, align_bytes=64)
        w2_scales = keep.tile([P, GROUPS, K_PASS], U8, align_bytes=64)
        rest_codes = keep.tile([P, GROUPS, FRAME_PIX], U32, align_bytes=64)
        rest_scales = keep.tile([P, GROUPS, FRAME_PIX], U8, align_bytes=64)

        hid_bias_rows = keep.tile([P, 2 * P], BF16)
        out_bias_rows = keep.tile([P, P], BF16)
        nc.vector.memset(hid_bias_rows[:], 0.0)
        nc.vector.memset(out_bias_rows[:], 0.0)
        nc.sync.dma_start(out=hid_bias_rows[0 : 2 * GROUPS, :], in_=conv_b.rearrange("(r c) -> r c", c=2 * P))
        nc.sync.dma_start(out=out_bias_rows[0:4, :], in_=conv_out_b.rearrange("(s c) -> s c", c=P))
        x_view = x.rearrange("b l (q e) h w -> q (b l) (e h w)", e=2)
        x_sb = keep.tile([P, FRAMES, 2 * 512], BF16)
        for first, last in ((0, 2), (2, FRAMES)):
            nc.sync.dma_start(out=x_sb[0:64, first:last, :], in_=x_view[:, first:last, :])
            nc.scalar.dma_start(out=x_sb[64:128, first:last, 0 : 2 * 512 - 16], in_=x_view[:, first:last, 16:])

        w1_view = conv_w.rearrange("(g u j e) k -> g j u (e k)", u=2, j=P, e=2)
        w2_view = conv_out_w.rearrange("(s m) (g o) -> g m s o", m=P, o=K_PASS)
        w1_words = {}
        w2_words = {}

        def exists(g):
            return 0 <= g < GROUPS

        def load_w1(g):
            if exists(g):
                w1_raw = raw.tile([P, 2, 2 * WAVE], BF16, tag="w1_raw")
                nc.sync.dma_start(out=w1_raw[:], in_=w1_view[g])
                w1_words[g] = w1_raw[:].bitcast(F32)

        def load_w2(g):
            if exists(g):
                w2_raw = raw.tile([P, 4, K_PASS], BF16, tag="w2_raw")
                nc.sync.dma_start(out=w2_raw[:], in_=w2_view[g])
                w2_words[g] = w2_raw[:].bitcast(F32)

        load_w1(0)
        for g in range(RAW_BUFS):
            if g + 1 < RAW_BUFS:
                load_w1(g + 1)
            load_w2(g)

        ident = keep.tile([P, P], F32)
        make_identity(nc, ident[:])
        row_sign = keep.tile([P, 1], F32)
        nc.vector.memset(row_sign[0:64], -1.0)
        nc.vector.memset(row_sign[64:128], 1.0)
        zero = keep.tile([P, 1], F32)
        nc.vector.memset(zero[:], 0.0)
        warm = keep.tile([P, 1], F32)
        nc.scalar.activation(out=warm[:], in_=zero[:], func=FUNC.Silu)

        pairs64 = keep.tile([P, 2, 64], F32)
        haar = keep.tile([P, 2, 192], BF16)
        for copy in range(2):
            nc.vector.tensor_add(out=pairs64[:, copy, :], in0=ident[:, 0:64], in1=ident[:, 64:128])
        pairs_flat = pairs64[:].rearrange("p r c -> p (r c)")
        for cols, factor in ((slice(0, 128), 0.5), (slice(128, 192), -0.5)):
            src = pairs_flat[:, 0 : cols.stop - cols.start]
            nc.vector.tensor_scalar_mul(out=haar[:, 0, cols], in0=src, scalar1=factor)
            nc.vector.tensor_scalar(
                out=haar[:, 1, cols], in0=src, scalar1=row_sign[:, 0:1], scalar2=factor, op0=ALU.mult, op1=ALU.mult
            )
        bias_f32 = keep.tile([P, 3, P], F32)
        nc.vector.tensor_copy(
            out=bias_f32[:, 0:2, :], in_=hid_bias_rows[:].rearrange("r (j e) -> r e j", e=2)
        )
        nc.vector.tensor_copy(out=bias_f32[:, 2, :], in_=out_bias_rows[:])
        bias_bank = work.tile([P, 3, P], F32, tag="work")
        for i in range(3):
            nc.tensor.transpose(bias_bank[:, i, :], bias_f32[:, i, :], ident[:])

        hid_bias = keep.tile([P, PACK * GROUPS], F32)
        out_bias_half = keep.tile([P, 4], F32)
        row_bias = keep.tile([P, 2], F32)
        nc.vector.tensor_copy(
            out=hid_bias[:].rearrange("j (r e) -> j r e", e=2),
            in_=bias_bank[:, 0:2, 0 : 2 * GROUPS].rearrange("j e r -> j r e"),
        )
        nc.vector.tensor_scalar_mul(out=out_bias_half[:], in0=bias_bank[:, 2, 0:4], scalar1=0.5)
        nc.vector.tensor_sub(out=row_bias[:, 0:1], in0=out_bias_half[:, 0:1], in1=out_bias_half[:, 2:3])
        nc.vector.tensor_add(out=row_bias[:, 1:2], in0=out_bias_half[:, 0:1], in1=out_bias_half[:, 2:3])

        for frame in range(FRAMES):
            bank = work.tile([P, PACK, FRAME_PIX], F32, tag="work")
            for u in range(2):
                for e in range(2):
                    x_even_rows = x_sb[:, frame, 512 * e : 512 * e + 512].rearrange(
                        "p (i a j b) -> p i a j b", a=2, j=8, b=2
                    )
                    for b in range(2):
                        nc.tensor.matmul(
                            out=bank[:, 2 * u + e, :].rearrange("p (i j) -> p i j", j=8),
                            lhsT=haar[:, u, 64 * (1 - b) : 64 * (1 - b) + P],
                            rhs=x_even_rows[:, :, 0, :, b],
                            start=(b == 0),
                            stop=(b == 1),
                        )
            dst = d_grouped[:, PACK * FRAME_PIX * frame : PACK * FRAME_PIX * (frame + 1)].rearrange(
                "p (n t) -> p n t", t=PACK
            )
            src = bank[:].rearrange("p t n -> p n t")
            if frame % 2 == 0:
                nc.vector.tensor_copy(out=dst, in_=src)
            else:
                nc.scalar.copy(out=dst, in_=src)

        w1_grouped = {}
        w2_grouped = {}
        w1_codes = {}
        w1_scales = {}
        hidden = {}
        hidden_r = {}
        f_grouped = {}
        fr_grouped = {}
        f_codes = {}
        f_scales = {}
        y_main = [acc.tile([P, PIX_MAIN], F32, name="y_main%d" % s) for s in range(4)]

        def transpose_512_columns(block, grouped, vector_helps):
            pairs = grouped[:].bitcast(F32).rearrange("p (c u) -> p c u", u=2)
            for half in range(2):
                bank = work.tile([P, 2, 2, P], F32, tag="work")
                for u in range(2):
                    for c in range(2):
                        nc.tensor.transpose(bank[:, u, c, :], block(half, u, c), ident[:])
                dst = pairs[:, 256 * half : 256 * half + 256, :]
                src = bank[:].rearrange("p u c j -> p (c j) u")
                if half == 1 and vector_helps:
                    nc.vector.tensor_copy(out=dst, in_=src)
                else:
                    nc.scalar.copy(out=dst, in_=src)

        def transpose_w1(g):
            if not exists(g):
                return
            w1_grouped[g] = ahead.tile([P, K_PASS * PACK], BF16, tag="w1_grouped", name="w1_grouped", bufs=2, align_bytes=64)
            words = w1_words[g]
            transpose_512_columns(
                lambda half, u, e: words[:, half, 256 * e + P * u : 256 * e + P * u + P],
                w1_grouped[g],
                g % 2 == 0,
            )
            load_w1(g + RAW_BUFS)

        def transpose_w2(g):
            if not exists(g):
                return
            w2_grouped[g] = ahead.tile([P, K_PASS * PACK], BF16, tag="w2_grouped", name="w2_grouped", bufs=2, align_bytes=64)
            words = w2_words[g]
            transpose_512_columns(
                lambda half, u, s: words[:, 2 * half + s, P * u : P * u + P], w2_grouped[g], True
            )
            load_w2(g + RAW_BUFS)

        def quantise_w1(g):
            if not exists(g):
                return
            w1_codes[g] = ahead.tile([P, K_PASS], U32, tag="w1_codes", name="w1_codes", align_bytes=64)
            w1_scales[g] = ahead.tile([P, K_PASS], U8, tag="w1_scales", name="w1_scales", align_bytes=64)
            nc.vector.quantize_mx(
                out=w1_codes[g][:].bitcast(FP8X4), scales=w1_scales[g][:], in_=w1_grouped[g][:]
            )

        def quantise_w2(g):
            if not exists(g):
                return
            nc.vector.quantize_mx(
                out=w2_codes[:, g, :].bitcast(FP8X4), scales=w2_scales[:, g, :], in_=w2_grouped[g][:]
            )

        def hidden_main(g, t):
            if not exists(g):
                return
            if t == 0:
                hidden[g] = stage.tile([P, PIX_MAIN // 8, PACK, 8], BF16, tag="hidden", name="hidden")
            bank = work.tile([P, PIX_MAIN], F32, tag="work")
            nc.tensor.matmul_mx(
                out=bank[:],
                lhsT=w1_codes[g][:, P * t : P * t + P].bitcast(FP8X4),
                lhsT_scale=w1_scales[g][:, P * t : P * t + P],
                rhs=d_codes[:, 0:PIX_MAIN].bitcast(FP8X4),
                rhs_scale=d_scales[:, 0:PIX_MAIN],
                start=True,
                stop=True,
            )
            nc.scalar.activation(
                out=hidden[g][:, :, t, :],
                in_=bank[:].rearrange("p (c i) -> p c i", i=8),
                func=FUNC.Silu,
                bias=hid_bias[:, PACK * g + t : PACK * g + t + 1],
                scale=1.0,
            )

        def hidden_rest(g):
            if not exists(g):
                return
            hidden_r[g] = stage.tile([P, FRAME_PIX // 8, PACK, 8], BF16, tag="hidden_r", name="hidden_r", bufs=3)
            bank = work.tile([P, PACK, FRAME_PIX], F32, tag="work")
            for t in range(PACK):
                nc.tensor.matmul_mx(
                    out=bank[:, t, :],
                    lhsT=w1_codes[g][:, P * t : P * t + P].bitcast(FP8X4),
                    lhsT_scale=w1_scales[g][:, P * t : P * t + P],
                    rhs=d_codes[:, PIX_MAIN:PIX].bitcast(FP8X4),
                    rhs_scale=d_scales[:, PIX_MAIN:PIX],
                    start=True,
                    stop=True,
                )
            for t in range(PACK):
                nc.scalar.activation(
                    out=hidden_r[g][:, :, t, :],
                    in_=bank[:, t, :].rearrange("p (c i) -> p c i", i=8),
                    func=FUNC.Silu,
                    bias=hid_bias[:, PACK * g + t : PACK * g + t + 1],
                    scale=1.0,
                )

        def regroup(copy, dst, src):
            copy(out=dst.rearrange("p (c i t) -> p c t i", i=8, t=PACK), in_=src)

        def main_tiles(g):
            f_grouped[g] = stage.tile([P, PIX_MAIN * PACK], BF16, tag="f_grouped", name="f_grouped", align_bytes=64)
            f_codes[g] = stage.tile([P, PIX_MAIN], U32, tag="f_codes", name="f_codes", bufs=3, align_bytes=64)
            f_scales[g] = stage.tile([P, PIX_MAIN], U8, tag="f_scales", name="f_scales", bufs=3, align_bytes=64)

        def regroup_main(g):
            if not exists(g):
                return
            main_tiles(g)
            regroup(nc.vector.tensor_copy, f_grouped[g][:], hidden[g][:])

        def regroup_rest(g):
            if not exists(g):
                return
            fr_grouped[g] = stage.tile([P, FRAME_PIX * PACK], BF16, tag="fr_grouped", name="fr_grouped", align_bytes=64)
            regroup(nc.vector.tensor_copy, fr_grouped[g][:], hidden_r[g][:])

        def quantise_main(g, first=0, last=PIX_MAIN):
            if not exists(g):
                return
            nc.vector.quantize_mx(
                out=f_codes[g][:, first:last].bitcast(FP8X4),
                scales=f_scales[g][:, first:last],
                in_=f_grouped[g][:, PACK * first : PACK * last],
            )

        def quantise_rest(g):
            if not exists(g):
                return
            nc.vector.quantize_mx(
                out=rest_codes[:, g, :].bitcast(FP8X4),
                scales=rest_scales[:, g, :],
                in_=fr_grouped[g][:],
            )

        def output_main(g, s, first=0, last=PIX_MAIN):
            if not exists(g):
                return
            nc.tensor.matmul_mx(
                out=y_main[s][:, first:last],
                lhsT=w2_codes[:, g, P * s : P * s + P].bitcast(FP8X4),
                lhsT_scale=w2_scales[:, g, P * s : P * s + P],
                rhs=f_codes[g][:, first:last].bitcast(FP8X4),
                rhs_scale=f_scales[g][:, first:last],
                start=(g == 0),
                stop=(g == GROUPS - 1),
            )

        transpose_w1(0)
        for first, last in ((0, PIX_MAIN), (PIX_MAIN, PIX)):
            nc.vector.quantize_mx(
                out=d_codes[:, first:last].bitcast(FP8X4),
                scales=d_scales[:, first:last],
                in_=d_grouped[:, PACK * first : PACK * last],
            )
        quantise_w1(0)
        transpose_w1(1)
        transpose_w2(0)
        quantise_w1(1)

        for step in range(GROUPS - 1):
            regroup_main(step - 1)
            hidden_main(step, 0)
            output_main(step - 2, 1)
            regroup_rest(step - 2)
            transpose_w1(step + 2)
            quantise_main(step - 1)
            quantise_w2(step)
            quantise_rest(step - 2)
            hidden_main(step, 1)
            output_main(step - 2, 0)
            hidden_main(step, 2)
            output_main(step - 2, 3)
            quantise_w1(step + 2)
            hidden_main(step, 3)
            output_main(step - 2, 2)
            transpose_w2(step + 1)
            hidden_rest(step - 1)

        tail = ctx.enter_context(tc.tile_pool(name="tail", bufs=1))
        z = tail.tile([P, 2, PIX], F32)
        low = tail.tile([P, 2, PIX], F32)
        high = tail.tile([P, 2, PIX], F32)
        image = tail.tile([P, FRAMES * 16, 2, 16], F32)
        out_view = out.rearrange("b l c h w -> c (b l) (h w)")
        image_view = image[:].rearrange("c (l i) a w -> c l (i a w)", l=FRAMES)

        def subband_pairs(first_frame, last_frame, banks):
            pix = slice(FRAME_PIX * first_frame, FRAME_PIX * last_frame)
            for r, pair in ((0, low), (1, high)):
                nc.scalar.activation(
                    out=z[:, r, pix],
                    in_=banks[2 * r + 1],
                    func=FUNC.Identity,
                    bias=out_bias_half[:, 2 * r + 1 : 2 * r + 2],
                    scale=0.5,
                )
                for b, op in ((0, ALU.subtract), (1, ALU.add)):
                    nc.vector.scalar_tensor_tensor(
                        out=pair[:, b, pix], in0=banks[2 * r], scalar=0.5, in1=z[:, r, pix], op0=ALU.mult, op1=op
                    )

        def rows_and_store(first_frame, last_frame):
            pix = slice(FRAME_PIX * first_frame, FRAME_PIX * last_frame)
            lines = slice(16 * first_frame, 16 * last_frame)
            for a, op in ((0, ALU.subtract), (1, ALU.add)):
                nc.vector.scalar_tensor_tensor(
                    out=image[:, lines, a, :].rearrange("c n (j b) -> c n j b", b=2),
                    in0=low[:, :, pix].rearrange("c b (n j) -> c n j b", j=8),
                    scalar=row_bias[:, a : a + 1],
                    in1=high[:, :, pix].rearrange("c b (n j) -> c n j b", j=8),
                    op0=ALU.add,
                    op1=op,
                )
            nc.sync.dma_start(
                out=out_view[:, first_frame:last_frame, :], in_=image_view[:, first_frame:last_frame, :]
            )

        LAST = GROUPS - 1
        HALF = PIX_MAIN // 2
        ORDER = (1, 0, 3, 2)
        y_rest = {}

        def output_rest(s, groups):
            if s not in y_rest:
                y_rest[s] = work.tile([P, FRAME_PIX], F32, tag="work", name="y_rest")
            for g in groups:
                nc.tensor.matmul_mx(
                    out=y_rest[s][:],
                    lhsT=w2_codes[:, g, P * s : P * s + P].bitcast(FP8X4),
                    lhsT_scale=w2_scales[:, g, P * s : P * s + P],
                    rhs=rest_codes[:, g, :].bitcast(FP8X4),
                    rhs_scale=rest_scales[:, g, :],
                    start=(g == 0),
                    stop=(g == LAST),
                )

        regroup_main(LAST - 1)
        hidden_main(LAST, 0)
        output_main(LAST - 2, 1)
        quantise_main(LAST - 1)
        quantise_w2(LAST)
        hidden_main(LAST, 1)
        output_main(LAST - 2, 0)
        hidden_main(LAST, 2)
        output_main(LAST - 2, 3)
        hidden_main(LAST, 3)
        output_main(LAST - 2, 2)
        main_tiles(LAST)
        blocks = HALF // 8
        regroup(nc.vector.tensor_copy, f_grouped[LAST][:, 0 : PACK * HALF], hidden[LAST][:, 0:blocks])
        regroup(nc.scalar.copy, f_grouped[LAST][:, PACK * HALF :], hidden[LAST][:, blocks:])
        hidden_rest(LAST - 1)
        hidden_rest(LAST)
        for s in ORDER:
            output_main(LAST - 1, s)
        regroup_rest(LAST - 2)
        quantise_main(LAST, 0, HALF)
        quantise_main(LAST, HALF, PIX_MAIN)
        quantise_rest(LAST - 2)
        for s in ORDER:
            output_main(LAST, s)
        regroup_rest(LAST - 1)
        regroup_rest(LAST)
        quantise_rest(LAST - 1)
        quantise_rest(LAST)
        subband_pairs(0, 4, [y_main[s][:] for s in range(4)])
        for s in ORDER:
            output_rest(s, range(LAST - 1))
        for s in ORDER:
            output_rest(s, range(LAST - 1, GROUPS))
        rows_and_store(0, 2)
        rows_and_store(2, 4)
        subband_pairs(4, 5, [y_rest[s][:] for s in range(4)])
        rows_and_store(4, 5)
